import numpy as np
import ml_dtypes


def mxq(x, axis, fmt="e4m3"):
    dtype, down = {"e4m3": (ml_dtypes.float8_e4m3fn, 7), "e5m2": (ml_dtypes.float8_e5m2, 14)}[fmt]
    v = np.moveaxis(np.asarray(x, np.float32).astype(ml_dtypes.bfloat16).astype(np.float64), axis, -1)
    blocks = v.reshape(v.shape[:-1] + (-1, 32))
    amax = np.abs(blocks).max(-1, keepdims=True)
    byte = np.maximum(np.where(amax > 0, np.frexp(amax)[1] - 1 + 127, 0) - down, 1)
    scale = np.exp2(byte - 127.0)
    codes = (blocks / scale).astype(np.float32).astype(dtype).astype(np.float64)
    return np.moveaxis((codes * scale).reshape(v.shape), -1, axis)


WIDE = False


def mx_kscale(k):
    if not WIDE:
        return np.ones(k)
    levels = np.array([10, -10, 5, -5, 0])
    a = np.random.permutation(np.resize(levels, k // 512 * 4)).reshape(k // 512, 4)
    idx = np.arange(k)
    return np.exp2(a[idx // 512, idx % 128 // 32])


BF16 = ml_dtypes.bfloat16


def bf(x):
    return np.asarray(x, np.float32).astype(BF16)


def f64(x):
    return np.asarray(x).astype(np.float64)


B, K, N, H, W = 1, 128, 128, 256, 256
NUM_ITERS = 5
TEMP = 0.1


def logsumexp(a, axis):
    m = a.max(axis=axis, keepdims=True)
    return m + np.log(np.exp(a - m).sum(axis=axis, keepdims=True))


def setup_inputs():
    s = mx_kscale(H * W).reshape(H, W)
    return {"pred_masks": bf(np.random.standard_normal((B, K, H, W)) * s),
            "gt_masks": bf(np.random.standard_normal((N, H, W)) * 0.5 / np.sqrt(H * W) / s)}


def reference(pred_masks, gt_masks):
    p = f64(pred_masks).reshape(B, K, H * W)
    g = f64(gt_masks).reshape(N, H * W)
    dot = mxq(p, 2, "e4m3") @ mxq(g, 1, "e4m3").T
    cost = 1.0 - dot
    log_alpha = -cost / TEMP
    for _ in range(NUM_ITERS):
        log_alpha = log_alpha - logsumexp(log_alpha, 2)
        log_alpha = log_alpha - logsumexp(log_alpha, 1)
    return np.exp(log_alpha)

@@ -1,0 +1,211 @@
+from contextlib import ExitStack
+
+import concourse.mybir as mybir
+from concourse.masks import make_identity
+
+FLOPS = 2 * 128 * 128 * 65536
+
+F32 = mybir.dt.float32
+BF16 = mybir.dt.bfloat16
+U32 = mybir.dt.uint32
+U8 = mybir.dt.uint8
+FP8X4 = mybir.dt.float8_e4m3fn_x4
+ALU = mybir.AluOpType
+ACT = mybir.ActivationFunctionType
+AX = mybir.AxisListType
+
+P = 128
+UNIT_K = 1024
+CHUNKS = [8, 8, 8, 8, 8, 8, 8, 4, 2, 1, 1]
+X_SLOTS = 9
+TAIL_FROM = 8
+MX_BATCH = 2
+ITERS = 5
+
+
+def tile_differentiablematcher_kernel(tc, pred_masks, gt_masks, out):
+    nc = tc.nc
+    srcs = {
+        "p": pred_masks.rearrange("b k h w -> (b k) (h w)"),
+        "g": gt_masks.rearrange("n h w -> n (h w)"),
+    }
+    out2 = out.rearrange("b k n -> (b k) n")
+
+    with ExitStack() as ctx:
+        ctx.enter_context(tc.manual_schedule())
+        const = ctx.enter_context(tc.tile_pool(name="const", bufs=1))
+        xin = ctx.enter_context(tc.tile_pool(name="xin", bufs=X_SLOTS))
+        grp = ctx.enter_context(tc.tile_pool(name="grp", bufs=4))
+        cq = ctx.enter_context(tc.tile_pool(name="cq", bufs=4))
+        psum = ctx.enter_context(tc.psum_pool(name="psum", bufs=7))
+        accp = ctx.enter_context(tc.psum_pool(name="accp", bufs=1))
+
+        starts = []
+        k0 = 0
+        for size in CHUNKS:
+            starts.append(k0)
+            k0 += size * UNIT_K
+        assert k0 == 65536
+        load_list = []
+        for c in range(len(CHUNKS)):
+            load_list.append(("p", c))
+            load_list.append(("g", c))
+        xt = {}
+        state = {"next_load": 0}
+
+        def load_next():
+            i = state["next_load"]
+            if i >= len(load_list):
+                return
+            state["next_load"] = i + 1
+            op, c = load_list[i]
+            width = CHUNKS[c] * UNIT_K
+            x = xin.tile([P, width], BF16, tag="x", name="x_%s%d" % (op, c))
+            nc.sync.dma_start(out=x[:], in_=srcs[op][:, starts[c] : starts[c] + width])
+            xt[(op, c)] = x
+
+        for i in range(X_SLOTS):
+            load_next()
+
+        ident = const.tile([P, P], F32, name="ident")
+        make_identity(nc, ident[:])
+        ones = const.tile([P, 1], F32, name="ones")
+        nc.vector.memset(ones[:], 1.0)
+        warm = const.tile([P, 1], F32, name="warm")
+        nc.scalar.activation(out=warm[:], in_=ones[:], func=ACT.Exp)
+
+        acc = accp.tile([P, P], F32, name="acc")
+
+        half_steps = []
+        n_ranges = 0
+        for c in range(len(CHUNKS)):
+            size = CHUNKS[c]
+            offs = list(range(0, size, 4))
+            for op in ("p", "g"):
+                for j in range(len(offs)):
+                    half_steps.append((op, c, offs[j], min(4, size - offs[j]), n_ranges + j))
+            n_ranges += len(offs)
+        total_passes = 65536 // 512
+
+        quantised = {}
+        mx_state = {"done": 0}
+
+        def transposes(h):
+            op, c, off, q, r = h
+            g = grp.tile([P, q * UNIT_K], BF16, tag="g", align_bytes=64, name="g_%s%d" % (op, r))
+            gw = g[:].bitcast(F32)
+            xw = xt[(op, c)][:].bitcast(F32)
+            for b in range(q):
+                bank = psum.tile([P, 512], F32, tag="bank", name="bank_%s%d_%d" % (op, r, b))
+                for j in range(4):
+                    col = 512 * (off + b) + 128 * j
+                    nc.tensor.transpose(bank[:, 128 * j : 128 * j + 128], xw[:, col : col + 128], ident[:])
+                dst = gw[:, 512 * b : 512 * b + 512].rearrange("p (g m u) -> p g m u", g=2, u=2)
+                src = bank[:].rearrange("p (g u m) -> p g m u", g=2, u=2)
+                if q > 1 and b == q - 1:
+                    nc.vector.tensor_copy(out=dst, in_=src)
+                else:
+                    nc.scalar.copy(out=dst, in_=src)
+            return g
+
+        def quantise(h, g):
+            op, c, off, q, r = h
+            codes = cq.tile([P, q * 256], U32, tag="c" + op, align_bytes=64, name="c_%s%d" % (op, r))
+            scales = cq.tile([P, q * 256], U8, tag="s" + op, align_bytes=64, name="s_%s%d" % (op, r))
+            nc.vector.quantize_mx(out=codes[:].bitcast(FP8X4), scales=scales[:], in_=g[:])
+            quantised[(op, r)] = (codes, scales, q)
+
+        def mx(r):
+            cp, sp, q = quantised[("p", r)]
+            cg, sg, q2 = quantised[("g", r)]
+            assert q == q2
+            for j in range(2 * q):
+                cols = slice(128 * j, 128 * j + 128)
+                n = mx_state["done"]
+                nc.tensor.matmul_mx(
+                    out=acc[:],
+                    lhsT=cp[:, cols].bitcast(FP8X4),
+                    lhsT_scale=sp[:, cols],
+                    rhs=cg[:, cols].bitcast(FP8X4),
+                    rhs_scale=sg[:, cols],
+                    start=(n == 0),
+                    stop=(n == total_passes - 1),
+                )
+                mx_state["done"] = n + 1
+
+        ready = []
+        issued = {"n": 0}
+        pending = []
+        for i in range(len(half_steps)):
+            h = half_steps[i]
+            op, c, off, q, r = h
+            tail = c >= TAIL_FROM
+            n_ready = len(ready)
+            g = transposes(h)
+            if off + q == CHUNKS[c]:
+                load_next()
+            if n_ready - issued["n"] >= (1 if tail else MX_BATCH):
+                for r2 in ready[issued["n"] : n_ready]:
+                    mx(r2)
+                issued["n"] = n_ready
+            todo = list(pending)
+            pending = []
+            if tail:
+                todo.append((h, g))
+            else:
+                pending.append((h, g))
+            for h2, g2 in todo:
+                quantise(h2, g2)
+                if h2[0] == "g":
+                    ready.append(h2[4])
+        for h2, g2 in pending:
+            quantise(h2, g2)
+            if h2[0] == "g":
+                ready.append(h2[4])
+        for r2 in ready[issued["n"] :]:
+            mx(r2)
+        assert mx_state["done"] == total_passes
+
+        mat = ctx.enter_context(tc.tile_pool(name="mat", bufs=1))
+        small = ctx.enter_context(tc.tile_pool(name="small", bufs=1))
+
+        m = small.tile([P, 1], F32, name="m")
+        nc.vector.reduce_max(out=m[:], in_=acc[:], axis=AX.X)
+        n1 = mat.tile([P, P], F32, name="n1")
+        nc.vector.tensor_scalar(
+            out=n1[:], in0=acc[:], scalar1=m[:, 0:1], scalar2=-10.0, op0=ALU.subtract, op1=ALU.mult
+        )
+        e1 = mat.tile([P, P], F32, name="e1")
+        a1 = small.tile([P, 1], F32, name="a1")
+        nc.scalar.activation(out=e1[:], in_=n1[:], func=ACT.Exp, scale=-1.0, accum_out=a1[:])
+        a_ps = a1
+        n1t = psum.tile([P, P], F32, tag="bank", name="n1t")
+        nc.tensor.transpose(n1t[:], n1[:], ident[:])
+        mu = small.tile([P, 1], F32, name="mu")
+        nc.vector.tensor_reduce(out=mu[:], in_=n1t[:], axis=AX.X, op=ALU.min)
+        kt = mat.tile([P, P], F32, name="kt")
+        nc.scalar.activation(out=kt[:], in_=n1t[:], func=ACT.Exp, bias=mu[:, 0:1], scale=-1.0)
+
+        k_ps = psum.tile([P, P], F32, tag="bank", name="k_ps")
+        nc.tensor.transpose(k_ps[:], kt[:], ident[:])
+        kk = mat.tile([P, P], F32, name="kk")
+        nc.scalar.copy(out=kk[:], in_=k_ps[:])
+        ku = mat.tile([P, P], F32, name="ku")
+        w = None
+        for it in range(ITERS):
+            u = small.tile([P, 1], F32, name="u%d" % it)
+            nc.vector.reciprocal(out=u[:], in_=a_ps[:])
+            c_ps = psum.tile([P, 1], F32, tag="bank", name="c_ps%d" % it)
+            nc.tensor.matmul(c_ps[:], lhsT=kk[:], rhs=u[:], start=True, stop=True)
+            if it == ITERS - 1:
+                nc.scalar.activation(out=ku[:], in_=kk[:], func=ACT.Copy, scale=u[:, 0:1])
+            w = small.tile([P, 1], F32, name="w%d" % it)
+            nc.vector.reciprocal(out=w[:], in_=c_ps[:])
+            if it < ITERS - 1:
+                a_ps = psum.tile([P, 1], F32, tag="bank", name="a_ps%d" % (it + 1))
+                nc.tensor.matmul(a_ps[:], lhsT=kt[:], rhs=w[:], start=True, stop=True)
+        wb = psum.tile([P, P], F32, tag="bank", name="wb")
+        nc.tensor.matmul(wb[:], lhsT=w[:, 0:1].to_broadcast([P, P]), rhs=ident[:], start=True, stop=True)
+        res = mat.tile([P, P], F32, name="res")
+        nc.vector.tensor_tensor(out=res[:], in0=ku[:], in1=wb[:], op=ALU.mult)
+        nc.sync.dma_start(out=out2, in_=res[:])

@@ -19,7 +19,8 @@ UNIT_K = 1024
 CHUNKS = [8, 8, 8, 8, 8, 8, 8, 4, 2, 1, 1]
 X_SLOTS = 9
 TAIL_FROM = 8
-MX_BATCH = 2
+GROUP = 4
+WARM = 12
 ITERS = 5
 
 
@@ -74,7 +75,27 @@ def tile_differentiablematcher_kernel(tc, pred_masks, gt_masks, out):
         warm = const.tile([P, 1], F32, name="warm")
         nc.scalar.activation(out=warm[:], in_=ones[:], func=ACT.Exp)
 
-        acc = accp.tile([P, P], F32, name="acc")
+        acc = accp.tile([P, 512], F32, name="acc")
+
+        dz = const.tile([P, 2048], BF16, name="dz", align_bytes=64)
+        nc.vector.memset(dz[:], 1.0)
+        dcodes = const.tile([P, 512], U32, name="dcodes", align_bytes=64)
+        dscales = const.tile([P, 512], U8, name="dscales", align_bytes=64)
+        nc.vector.quantize_mx(out=dcodes[:].bitcast(FP8X4), scales=dscales[:], in_=dz[:])
+
+        def dummy(n):
+            for i in range(n):
+                nc.tensor.matmul_mx(
+                    out=acc[:],
+                    lhsT=dcodes[:, 0:128].bitcast(FP8X4),
+                    lhsT_scale=dscales[:, 0:128],
+                    rhs=dcodes[:].bitcast(FP8X4),
+                    rhs_scale=dscales[:],
+                    start=True,
+                    stop=True,
+                )
+
+        dummy(WARM)
 
         half_steps = []
         n_ranges = 0
@@ -115,27 +136,32 @@ def tile_differentiablematcher_kernel(tc, pred_masks, gt_masks, out):
             nc.vector.quantize_mx(out=codes[:].bitcast(FP8X4), scales=scales[:], in_=g[:])
             quantised[(op, r)] = (codes, scales, q)
 
-        def mx(r):
+        def mx_pass(r, j, wide):
             cp, sp, q = quantised[("p", r)]
             cg, sg, q2 = quantised[("g", r)]
             assert q == q2
-            for j in range(2 * q):
-                cols = slice(128 * j, 128 * j + 128)
-                n = mx_state["done"]
-                nc.tensor.matmul_mx(
-                    out=acc[:],
-                    lhsT=cp[:, cols].bitcast(FP8X4),
-                    lhsT_scale=sp[:, cols],
-                    rhs=cg[:, cols].bitcast(FP8X4),
-                    rhs_scale=sg[:, cols],
-                    start=(n == 0),
-                    stop=(n == total_passes - 1),
-                )
-                mx_state["done"] = n + 1
+            width = 256 if (wide and j % 2 == 0) else 128
+            n = mx_state["done"]
+            nc.tensor.matmul_mx(
+                out=acc[:, 0:width],
+                lhsT=cp[:, 128 * j : 128 * j + 128].bitcast(FP8X4),
+                lhsT_scale=sp[:, 128 * j : 128 * j + 128],
+                rhs=cg[:, 128 * j : 128 * j + width].bitcast(FP8X4),
+                rhs_scale=sg[:, 128 * j : 128 * j + width],
+                start=(n == 0),
+                stop=(n == total_passes - 1),
+            )
+            mx_state["done"] = n + 1
 
         ready = []
         issued = {"n": 0}
         pending = []
+
+        def note_ready(h2):
+            if h2[0] == "g":
+                for j in range(2 * h2[3]):
+                    ready.append((h2[4], j))
+
         for i in range(len(half_steps)):
             h = half_steps[i]
             op, c, off, q, r = h
@@ -144,10 +170,13 @@ def tile_differentiablematcher_kernel(tc, pred_masks, gt_masks, out):
             g = transposes(h)
             if off + q == CHUNKS[c]:
                 load_next()
-            if n_ready - issued["n"] >= (1 if tail else MX_BATCH):
-                for r2 in ready[issued["n"] : n_ready]:
-                    mx(r2)
-                issued["n"] = n_ready
+            first = issued["n"]
+            last = n_ready if tail else min(n_ready, first + GROUP)
+            if last == 0:
+                dummy(2)
+            for r2, j2 in ready[first:last]:
+                mx_pass(r2, j2, not tail)
+            issued["n"] = last
             todo = list(pending)
             pending = []
             if tail:
@@ -156,24 +185,22 @@ def tile_differentiablematcher_kernel(tc, pred_masks, gt_masks, out):
                 pending.append((h, g))
             for h2, g2 in todo:
                 quantise(h2, g2)
-                if h2[0] == "g":
-                    ready.append(h2[4])
+                note_ready(h2)
         for h2, g2 in pending:
             quantise(h2, g2)
-            if h2[0] == "g":
-                ready.append(h2[4])
-        for r2 in ready[issued["n"] :]:
-            mx(r2)
+            note_ready(h2)
+        for r2, j2 in ready[issued["n"] :]:
+            mx_pass(r2, j2, False)
         assert mx_state["done"] == total_passes
 
         mat = ctx.enter_context(tc.tile_pool(name="mat", bufs=1))
         small = ctx.enter_context(tc.tile_pool(name="small", bufs=1))
 
         m = small.tile([P, 1], F32, name="m")
-        nc.vector.reduce_max(out=m[:], in_=acc[:], axis=AX.X)
+        nc.vector.reduce_max(out=m[:], in_=acc[:, 0:P], axis=AX.X)
         n1 = mat.tile([P, P], F32, name="n1")
         nc.vector.tensor_scalar(
-            out=n1[:], in0=acc[:], scalar1=m[:, 0:1], scalar2=-10.0, op0=ALU.subtract, op1=ALU.mult
+            out=n1[:], in0=acc[:, 0:P], scalar1=m[:, 0:1], scalar2=-10.0, op0=ALU.subtract, op1=ALU.mult
         )
         e1 = mat.tile([P, P], F32, name="e1")
         a1 = small.tile([P, 1], F32, name="a1")

@@ -196,6 +196,11 @@ def tile_differentiablematcher_kernel(tc, pred_masks, gt_masks, out):
         mat = ctx.enter_context(tc.tile_pool(name="mat", bufs=1))
         small = ctx.enter_context(tc.tile_pool(name="small", bufs=1))
 
+        def spread(vec, name):
+            t = psum.tile([P, P], F32, tag="bank", name=name)
+            nc.tensor.transpose(t[:], vec[:, 0:1].to_broadcast([P, P]), ident[:])
+            return t
+
         m = small.tile([P, 1], F32, name="m")
         nc.vector.reduce_max(out=m[:], in_=acc[:, 0:P], axis=AX.X)
         n1 = mat.tile([P, P], F32, name="n1")
@@ -205,34 +210,39 @@ def tile_differentiablematcher_kernel(tc, pred_masks, gt_masks, out):
         e1 = mat.tile([P, P], F32, name="e1")
         a1 = small.tile([P, 1], F32, name="a1")
         nc.scalar.activation(out=e1[:], in_=n1[:], func=ACT.Exp, scale=-1.0, accum_out=a1[:])
-        a_ps = a1
         n1t = psum.tile([P, P], F32, tag="bank", name="n1t")
         nc.tensor.transpose(n1t[:], n1[:], ident[:])
         mu = small.tile([P, 1], F32, name="mu")
         nc.vector.tensor_reduce(out=mu[:], in_=n1t[:], axis=AX.X, op=ALU.min)
         kt = mat.tile([P, P], F32, name="kt")
         nc.scalar.activation(out=kt[:], in_=n1t[:], func=ACT.Exp, bias=mu[:, 0:1], scale=-1.0)
+        u = small.tile([P, 1], F32, name="u0")
+        nc.vector.reciprocal(out=u[:], in_=a1[:])
+        ub = spread(u, "ub")
+        ktu = mat.tile([P, P], F32, name="ktu")
+        c1 = small.tile([P, 1], F32, name="c1")
+        nc.vector.scalar_tensor_tensor(
+            out=ktu[:], in0=kt[:], scalar=1.0, in1=ub[:], op0=ALU.mult, op1=ALU.mult, accum_out=c1[:]
+        )
+        w = small.tile([P, 1], F32, name="w0")
+        nc.vector.reciprocal(out=w[:], in_=c1[:])
 
         k_ps = psum.tile([P, P], F32, tag="bank", name="k_ps")
         nc.tensor.transpose(k_ps[:], kt[:], ident[:])
         kk = mat.tile([P, P], F32, name="kk")
         nc.scalar.copy(out=kk[:], in_=k_ps[:])
-        ku = mat.tile([P, P], F32, name="ku")
-        w = None
-        for it in range(ITERS):
+        for it in range(1, ITERS):
+            a_ps = psum.tile([P, 1], F32, tag="bank", name="a_ps%d" % it)
+            nc.tensor.matmul(a_ps[:], lhsT=kt[:], rhs=w[:], start=True, stop=True)
             u = small.tile([P, 1], F32, name="u%d" % it)
             nc.vector.reciprocal(out=u[:], in_=a_ps[:])
             c_ps = psum.tile([P, 1], F32, tag="bank", name="c_ps%d" % it)
             nc.tensor.matmul(c_ps[:], lhsT=kk[:], rhs=u[:], start=True, stop=True)
-            if it == ITERS - 1:
-                nc.scalar.activation(out=ku[:], in_=kk[:], func=ACT.Copy, scale=u[:, 0:1])
             w = small.tile([P, 1], F32, name="w%d" % it)
             nc.vector.reciprocal(out=w[:], in_=c_ps[:])
-            if it < ITERS - 1:
-                a_ps = psum.tile([P, 1], F32, tag="bank", name="a_ps%d" % (it + 1))
-                nc.tensor.matmul(a_ps[:], lhsT=kt[:], rhs=w[:], start=True, stop=True)
-        wb = psum.tile([P, P], F32, tag="bank", name="wb")
-        nc.tensor.matmul(wb[:], lhsT=w[:, 0:1].to_broadcast([P, P]), rhs=ident[:], start=True, stop=True)
+        wb = spread(w, "wb")
         res = mat.tile([P, P], F32, name="res")
-        nc.vector.tensor_tensor(out=res[:], in0=ku[:], in1=wb[:], op=ALU.mult)
+        nc.vector.scalar_tensor_tensor(
+            out=res[:], in0=kk[:], scalar=u[:, 0:1], in1=wb[:], op0=ALU.mult, op1=ALU.mult
+        )
         nc.sync.dma_start(out=out2, in_=res[:])

@@ -15,12 +15,13 @@ ACT = mybir.ActivationFunctionType
 AX = mybir.AxisListType
 
 P = 128
-UNIT_K = 1024
-CHUNKS = [8, 8, 8, 8, 8, 8, 8, 4, 2, 1, 1]
-X_SLOTS = 9
-TAIL_FROM = 8
-GROUP = 4
-WARM = 12
+K_TOTAL = 65536
+PASS_K = 512
+CHUNKS = [16, 16, 16, 16, 16, 12, 8, 8, 6, 4, 4, 2, 2, 1, 1]
+X_SLOTS = 8
+GROUP_SIZES = (8, 4, 2, 1)
+CODE_BUFS = {("p", 8): 4, ("g", 8): 3}
+MX_LAG_BANKS = 8
 ITERS = 5
 
 
@@ -31,13 +32,17 @@ def tile_differentiablematcher_kernel(tc, pred_masks, gt_masks, out):
         "g": gt_masks.rearrange("n h w -> n (h w)"),
     }
     out2 = out.rearrange("b k n -> (b k) n")
+    total_passes = K_TOTAL // PASS_K
+    assert sum(CHUNKS) == total_passes
 
     with ExitStack() as ctx:
         ctx.enter_context(tc.manual_schedule())
         const = ctx.enter_context(tc.tile_pool(name="const", bufs=1))
         xin = ctx.enter_context(tc.tile_pool(name="xin", bufs=X_SLOTS))
         grp = ctx.enter_context(tc.tile_pool(name="grp", bufs=4))
-        cq = ctx.enter_context(tc.tile_pool(name="cq", bufs=4))
+        cq = ctx.enter_context(tc.tile_pool(name="cq", bufs=3))
+        mat = ctx.enter_context(tc.tile_pool(name="mat", bufs=1))
+        small = ctx.enter_context(tc.tile_pool(name="small", bufs=1))
         psum = ctx.enter_context(tc.psum_pool(name="psum", bufs=7))
         accp = ctx.enter_context(tc.psum_pool(name="accp", bufs=1))
 
@@ -45,14 +50,13 @@ def tile_differentiablematcher_kernel(tc, pred_masks, gt_masks, out):
         k0 = 0
         for size in CHUNKS:
             starts.append(k0)
-            k0 += size * UNIT_K
-        assert k0 == 65536
+            k0 += size * PASS_K
         load_list = []
         for c in range(len(CHUNKS)):
             load_list.append(("p", c))
             load_list.append(("g", c))
         xt = {}
-        state = {"next_load": 0}
+        state = {"next_load": 0, "banks": 0, "done": 0, "issued": 0, "s": 0, "v": 0}
 
         def load_next():
             i = state["next_load"]
@@ -60,7 +64,7 @@ def tile_differentiablematcher_kernel(tc, pred_masks, gt_masks, out):
                 return
             state["next_load"] = i + 1
             op, c = load_list[i]
-            width = CHUNKS[c] * UNIT_K
+            width = CHUNKS[c] * PASS_K
             x = xin.tile([P, width], BF16, tag="x", name="x_%s%d" % (op, c))
             nc.sync.dma_start(out=x[:], in_=srcs[op][:, starts[c] : starts[c] + width])
             xt[(op, c)] = x
@@ -75,126 +79,99 @@ def tile_differentiablematcher_kernel(tc, pred_masks, gt_masks, out):
         warm = const.tile([P, 1], F32, name="warm")
         nc.scalar.activation(out=warm[:], in_=ones[:], func=ACT.Exp)
 
-        acc = accp.tile([P, 512], F32, name="acc")
+        acc = accp.tile([P, P], F32, name="acc")
 
-        dz = const.tile([P, 2048], BF16, name="dz", align_bytes=64)
-        nc.vector.memset(dz[:], 1.0)
-        dcodes = const.tile([P, 512], U32, name="dcodes", align_bytes=64)
-        dscales = const.tile([P, 512], U8, name="dscales", align_bytes=64)
-        nc.vector.quantize_mx(out=dcodes[:].bitcast(FP8X4), scales=dscales[:], in_=dz[:])
-
-        def dummy(n):
-            for i in range(n):
-                nc.tensor.matmul_mx(
-                    out=acc[:],
-                    lhsT=dcodes[:, 0:128].bitcast(FP8X4),
-                    lhsT_scale=dscales[:, 0:128],
-                    rhs=dcodes[:].bitcast(FP8X4),
-                    rhs_scale=dscales[:],
-                    start=True,
-                    stop=True,
-                )
-
-        dummy(WARM)
-
-        half_steps = []
+        groups = []
         n_ranges = 0
         for c in range(len(CHUNKS)):
-            size = CHUNKS[c]
-            offs = list(range(0, size, 4))
+            parts = []
+            off = 0
+            for q in GROUP_SIZES:
+                while CHUNKS[c] - off >= q:
+                    parts.append((off, q))
+                    off += q
             for op in ("p", "g"):
-                for j in range(len(offs)):
-                    half_steps.append((op, c, offs[j], min(4, size - offs[j]), n_ranges + j))
-            n_ranges += len(offs)
-        total_passes = 65536 // 512
+                for j in range(len(parts)):
+                    off, q = parts[j]
+                    groups.append((op, c, off, q, n_ranges + j, j == len(parts) - 1))
+            n_ranges += len(parts)
 
         quantised = {}
-        mx_state = {"done": 0}
+        ready = []
 
         def transposes(h):
-            op, c, off, q, r = h
-            g = grp.tile([P, q * UNIT_K], BF16, tag="g", align_bytes=64, name="g_%s%d" % (op, r))
+            op, c, off, q, r, last = h
+            g = grp.tile([P, q * PASS_K], BF16, tag="g", align_bytes=64, name="g_%s%d" % (op, r))
             gw = g[:].bitcast(F32)
             xw = xt[(op, c)][:].bitcast(F32)
-            for b in range(q):
+            state["v"] += 2 * q + 2
+            for b in range((q + 1) // 2):
+                n = min(2, q - 2 * b)
                 bank = psum.tile([P, 512], F32, tag="bank", name="bank_%s%d_%d" % (op, r, b))
-                for j in range(4):
-                    col = 512 * (off + b) + 128 * j
+                for j in range(2 * n):
+                    col = 256 * (off + 2 * b) + 128 * j
                     nc.tensor.transpose(bank[:, 128 * j : 128 * j + 128], xw[:, col : col + 128], ident[:])
-                dst = gw[:, 512 * b : 512 * b + 512].rearrange("p (g m u) -> p g m u", g=2, u=2)
-                src = bank[:].rearrange("p (g u m) -> p g m u", g=2, u=2)
-                if q > 1 and b == q - 1:
+                state["banks"] += 1
+                dst = gw[:, 512 * b : 512 * b + 256 * n].rearrange("p (s m u) -> p s m u", s=n, u=2)
+                src = bank[:, 0 : 256 * n].rearrange("p (s u m) -> p s m u", s=n, u=2)
+                if state["v"] < state["s"]:
+                    state["v"] += 4 * n + 1
                     nc.vector.tensor_copy(out=dst, in_=src)
                 else:
+                    state["s"] += 4 * n + 1
                     nc.scalar.copy(out=dst, in_=src)
             return g
 
         def quantise(h, g):
-            op, c, off, q, r = h
-            codes = cq.tile([P, q * 256], U32, tag="c" + op, align_bytes=64, name="c_%s%d" % (op, r))
-            scales = cq.tile([P, q * 256], U8, tag="s" + op, align_bytes=64, name="s_%s%d" % (op, r))
-            nc.vector.quantize_mx(out=codes[:].bitcast(FP8X4), scales=scales[:], in_=g[:])
-            quantised[(op, r)] = (codes, scales, q)
-
-        def mx_pass(r, j, wide):
-            cp, sp, q = quantised[("p", r)]
-            cg, sg, q2 = quantised[("g", r)]
-            assert q == q2
-            width = 256 if (wide and j % 2 == 0) else 128
-            n = mx_state["done"]
-            nc.tensor.matmul_mx(
-                out=acc[:, 0:width],
-                lhsT=cp[:, 128 * j : 128 * j + 128].bitcast(FP8X4),
-                lhsT_scale=sp[:, 128 * j : 128 * j + 128],
-                rhs=cg[:, 128 * j : 128 * j + width].bitcast(FP8X4),
-                rhs_scale=sg[:, 128 * j : 128 * j + width],
-                start=(n == 0),
-                stop=(n == total_passes - 1),
+            op, c, off, q, r, last = h
+            bufs = CODE_BUFS.get((op, q), 3)
+            codes = cq.tile(
+                [P, q * P], U32, tag="c%s%d" % (op, q), bufs=bufs, align_bytes=64, name="c_%s%d" % (op, r)
             )
-            mx_state["done"] = n + 1
+            scales = cq.tile(
+                [P, q * P], U8, tag="s%s%d" % (op, q), bufs=bufs, align_bytes=64, name="s_%s%d" % (op, r)
+            )
+            nc.vector.quantize_mx(out=codes[:].bitcast(FP8X4), scales=scales[:], in_=g[:])
+            quantised[(op, r)] = (codes, scales)
+            if op == "g":
+                for j in range(q):
+                    ready.append((r, j, state["banks"]))
 
-        ready = []
-        issued = {"n": 0}
-        pending = []
+        def mx_passes(count):
+            first = state["issued"]
+            for r, j, b in ready[first : first + count]:
+                cp, sp = quantised[("p", r)]
+                cg, sg = quantised[("g", r)]
+                cols = slice(P * j, P * j + P)
+                n = state["done"]
+                nc.tensor.matmul_mx(
+                    out=acc[:],
+                    lhsT=cp[:, cols].bitcast(FP8X4),
+                    lhsT_scale=sp[:, cols],
+                    rhs=cg[:, cols].bitcast(FP8X4),
+                    rhs_scale=sg[:, cols],
+                    start=(n == 0),
+                    stop=(n == total_passes - 1),
+                )
+                state["done"] = n + 1
+            state["issued"] = first + count
 
-        def note_ready(h2):
-            if h2[0] == "g":
-                for j in range(2 * h2[3]):
-                    ready.append((h2[4], j))
-
-        for i in range(len(half_steps)):
-            h = half_steps[i]
-            op, c, off, q, r = h
-            tail = c >= TAIL_FROM
-            n_ready = len(ready)
+        waiting = None
+        for h in groups:
             g = transposes(h)
-            if off + q == CHUNKS[c]:
+            if h[5]:
                 load_next()
-            first = issued["n"]
-            last = n_ready if tail else min(n_ready, first + GROUP)
-            if last == 0:
-                dummy(2)
-            for r2, j2 in ready[first:last]:
-                mx_pass(r2, j2, not tail)
-            issued["n"] = last
-            todo = list(pending)
-            pending = []
-            if tail:
-                todo.append((h, g))
-            else:
-                pending.append((h, g))
-            for h2, g2 in todo:
-                quantise(h2, g2)
-                note_ready(h2)
-        for h2, g2 in pending:
-            quantise(h2, g2)
-            note_ready(h2)
-        for r2, j2 in ready[issued["n"] :]:
-            mx_pass(r2, j2, False)
-        assert mx_state["done"] == total_passes
-
-        mat = ctx.enter_context(tc.tile_pool(name="mat", bufs=1))
-        small = ctx.enter_context(tc.tile_pool(name="small", bufs=1))
+            count = 0
+            for r, j, b in ready[state["issued"] :]:
+                if state["banks"] - b >= MX_LAG_BANKS:
+                    count += 1
+            mx_passes(count)
+            if waiting is not None:
+                quantise(waiting[0], waiting[1])
+            waiting = (h, g)
+        quantise(waiting[0], waiting[1])
+        mx_passes(len(ready) - state["issued"])
+        assert state["done"] == total_passes
 
         def spread(vec, name):
             t = psum.tile([P, P], F32, tag="bank", name=name)
@@ -202,10 +179,10 @@ def tile_differentiablematcher_kernel(tc, pred_masks, gt_masks, out):
             return t
 
         m = small.tile([P, 1], F32, name="m")
-        nc.vector.reduce_max(out=m[:], in_=acc[:, 0:P], axis=AX.X)
+        nc.vector.reduce_max(out=m[:], in_=acc[:], axis=AX.X)
         n1 = mat.tile([P, P], F32, name="n1")
         nc.vector.tensor_scalar(
-            out=n1[:], in0=acc[:, 0:P], scalar1=m[:, 0:1], scalar2=-10.0, op0=ALU.subtract, op1=ALU.mult
+            out=n1[:], in0=acc[:], scalar1=m[:, 0:1], scalar2=-10.0, op0=ALU.subtract, op1=ALU.mult
         )
         e1 = mat.tile([P, P], F32, name="e1")
         a1 = small.tile([P, 1], F32, name="a1")

@@ -17,10 +17,10 @@ AX = mybir.AxisListType
 P = 128
 K_TOTAL = 65536
 PASS_K = 512
-CHUNKS = [16, 16, 16, 16, 16, 12, 8, 8, 6, 4, 4, 2, 2, 1, 1]
+CHUNKS = [16, 16, 12, 12, 12, 12, 12, 8, 6, 6, 4, 4, 4, 2, 2]
 X_SLOTS = 8
 GROUP_SIZES = (8, 4, 2, 1)
-CODE_BUFS = {("p", 8): 4, ("g", 8): 3}
+CODE_BUFS = {("p", 8): 4, ("p", 4): 4, ("g", 4): 4}
 MX_LAG_BANKS = 8
 ITERS = 5
 
@@ -189,13 +189,13 @@ def tile_differentiablematcher_kernel(tc, pred_masks, gt_masks, out):
         nc.scalar.activation(out=e1[:], in_=n1[:], func=ACT.Exp, scale=-1.0, accum_out=a1[:])
         n1t = psum.tile([P, P], F32, tag="bank", name="n1t")
         nc.tensor.transpose(n1t[:], n1[:], ident[:])
+        u = small.tile([P, 1], F32, name="u0")
+        nc.vector.reciprocal(out=u[:], in_=a1[:])
+        ub = spread(u, "ub")
         mu = small.tile([P, 1], F32, name="mu")
         nc.vector.tensor_reduce(out=mu[:], in_=n1t[:], axis=AX.X, op=ALU.min)
         kt = mat.tile([P, P], F32, name="kt")
         nc.scalar.activation(out=kt[:], in_=n1t[:], func=ACT.Exp, bias=mu[:, 0:1], scale=-1.0)
-        u = small.tile([P, 1], F32, name="u0")
-        nc.vector.reciprocal(out=u[:], in_=a1[:])
-        ub = spread(u, "ub")
         ktu = mat.tile([P, P], F32, name="ktu")
         c1 = small.tile([P, 1], F32, name="c1")
         nc.vector.scalar_tensor_tensor(

@@ -17,10 +17,10 @@ AX = mybir.AxisListType
 P = 128
 K_TOTAL = 65536
 PASS_K = 512
-CHUNKS = [16, 16, 12, 12, 12, 12, 12, 8, 6, 6, 4, 4, 4, 2, 2]
+CHUNKS = [16, 16, 16, 16, 16, 12, 8, 8, 6, 4, 4, 2, 2, 1, 1]
 X_SLOTS = 8
 GROUP_SIZES = (8, 4, 2, 1)
-CODE_BUFS = {("p", 8): 4, ("p", 4): 4, ("g", 4): 4}
+CODE_BUFS = {("p", 8): 4, ("g", 8): 3}
 MX_LAG_BANKS = 8
 ITERS = 5
 
@@ -56,7 +56,7 @@ def tile_differentiablematcher_kernel(tc, pred_masks, gt_masks, out):
             load_list.append(("p", c))
             load_list.append(("g", c))
         xt = {}
-        state = {"next_load": 0, "banks": 0, "done": 0, "issued": 0, "s": 0, "v": 0}
+        state = {"next_load": 0, "banks": 0, "done": 0, "issued": 0, "s": 0, "v": 0, "dummies": 0}
 
         def load_next():
             i = state["next_load"]
@@ -80,6 +80,11 @@ def tile_differentiablematcher_kernel(tc, pred_masks, gt_masks, out):
         nc.scalar.activation(out=warm[:], in_=ones[:], func=ACT.Exp)
 
         acc = accp.tile([P, P], F32, name="acc")
+        dz = const.tile([P, 2048], BF16, name="dz", align_bytes=64)
+        nc.vector.memset(dz[:], 1.0)
+        dcodes = const.tile([P, 512], U32, name="dcodes", align_bytes=64)
+        dscales = const.tile([P, 512], U8, name="dscales", align_bytes=64)
+        nc.vector.quantize_mx(out=dcodes[:].bitcast(FP8X4), scales=dscales[:], in_=dz[:])
 
         groups = []
         n_ranges = 0
@@ -156,6 +161,20 @@ def tile_differentiablematcher_kernel(tc, pred_masks, gt_masks, out):
                 state["done"] = n + 1
             state["issued"] = first + count
 
+        def dummy(widths):
+            state["dummies"] += 1
+            scratch = psum.tile([P, 512], F32, tag="bank", name="scratch%d" % state["dummies"])
+            for width in widths:
+                nc.tensor.matmul_mx(
+                    out=scratch[:, 0:width],
+                    lhsT=dcodes[:, 0:128].bitcast(FP8X4),
+                    lhsT_scale=dscales[:, 0:128],
+                    rhs=dcodes[:, 0:width].bitcast(FP8X4),
+                    rhs_scale=dscales[:, 0:width],
+                    start=True,
+                    stop=True,
+                )
+
         waiting = None
         for h in groups:
             g = transposes(h)
@@ -170,8 +189,12 @@ def tile_differentiablematcher_kernel(tc, pred_masks, gt_masks, out):
                 quantise(waiting[0], waiting[1])
             waiting = (h, g)
         quantise(waiting[0], waiting[1])
-        mx_passes(len(ready) - state["issued"])
+        mx_passes(len(ready) - state["issued"] - waiting[0][3])
+        dummy((512, 256))
+        mx_passes(waiting[0][3])
         assert state["done"] == total_passes
+
+        dummy((512, 256))
 
         def spread(vec, name):
             t = psum.tile([P, P], F32, tag="bank", name=name)
@@ -189,9 +212,11 @@ def tile_differentiablematcher_kernel(tc, pred_masks, gt_masks, out):
         nc.scalar.activation(out=e1[:], in_=n1[:], func=ACT.Exp, scale=-1.0, accum_out=a1[:])
         n1t = psum.tile([P, P], F32, tag="bank", name="n1t")
         nc.tensor.transpose(n1t[:], n1[:], ident[:])
+        dummy((512,))
         u = small.tile([P, 1], F32, name="u0")
         nc.vector.reciprocal(out=u[:], in_=a1[:])
         ub = spread(u, "ub")
+        dummy((512,))
         mu = small.tile([P, 1], F32, name="mu")
         nc.vector.tensor_reduce(out=mu[:], in_=n1t[:], axis=AX.X, op=ALU.min)
         kt = mat.tile([P, P], F32, name="kt")
@@ -206,15 +231,18 @@ def tile_differentiablematcher_kernel(tc, pred_masks, gt_masks, out):
 
         k_ps = psum.tile([P, P], F32, tag="bank", name="k_ps")
         nc.tensor.transpose(k_ps[:], kt[:], ident[:])
+        dummy((512,))
         kk = mat.tile([P, P], F32, name="kk")
         nc.scalar.copy(out=kk[:], in_=k_ps[:])
         for it in range(1, ITERS):
             a_ps = psum.tile([P, 1], F32, tag="bank", name="a_ps%d" % it)
             nc.tensor.matmul(a_ps[:], lhsT=kt[:], rhs=w[:], start=True, stop=True)
+            dummy((512, 256))
             u = small.tile([P, 1], F32, name="u%d" % it)
             nc.vector.reciprocal(out=u[:], in_=a_ps[:])
             c_ps = psum.tile([P, 1], F32, tag="bank", name="c_ps%d" % it)
             nc.tensor.matmul(c_ps[:], lhsT=kk[:], rhs=u[:], start=True, stop=True)
+            dummy((512, 256))
             w = small.tile([P, 1], F32, name="w%d" % it)
             nc.vector.reciprocal(out=w[:], in_=c_ps[:])
         wb = spread(w, "wb")

@@ -18,7 +18,8 @@ P = 128
 K_TOTAL = 65536
 PASS_K = 512
 CHUNKS = [16, 16, 16, 16, 16, 12, 8, 8, 6, 4, 4, 2, 2, 1, 1]
-X_SLOTS = 8
+X_SLOTS = 6
+SMALL = 4
 GROUP_SIZES = (8, 4, 2, 1)
 CODE_BUFS = {("p", 8): 4, ("g", 8): 3}
 MX_LAG_BANKS = 8
@@ -58,16 +59,23 @@ def tile_differentiablematcher_kernel(tc, pred_masks, gt_masks, out):
         xt = {}
         state = {"next_load": 0, "banks": 0, "done": 0, "issued": 0, "s": 0, "v": 0, "dummies": 0}
 
-        def load_next():
+        def load_one():
             i = state["next_load"]
-            if i >= len(load_list):
-                return
             state["next_load"] = i + 1
             op, c = load_list[i]
             width = CHUNKS[c] * PASS_K
-            x = xin.tile([P, width], BF16, tag="x", name="x_%s%d" % (op, c))
+            if CHUNKS[c] > SMALL:
+                x = xin.tile([P, width], BF16, tag="x", name="x_%s%d" % (op, c))
+            else:
+                x = xin.tile([P, width], BF16, tag="x_%s%d" % (op, c), bufs=1, name="x_%s%d" % (op, c))
             nc.sync.dma_start(out=x[:], in_=srcs[op][:, starts[c] : starts[c] + width])
             xt[(op, c)] = x
+
+        def load_next():
+            if state["next_load"] < len(load_list):
+                load_one()
+            while state["next_load"] < len(load_list) and CHUNKS[load_list[state["next_load"]][1]] <= SMALL:
+                load_one()
 
         for i in range(X_SLOTS):
             load_next()

@@ -117,7 +117,7 @@ def tile_differentiablematcher_kernel(tc, pred_masks, gt_masks, out):
             g = grp.tile([P, q * PASS_K], BF16, tag="g", align_bytes=64, name="g_%s%d" % (op, r))
             gw = g[:].bitcast(F32)
             xw = xt[(op, c)][:].bitcast(F32)
-            state["v"] += 2 * q + 2
+            state["v"] += 5 * q + 2
             for b in range((q + 1) // 2):
                 n = min(2, q - 2 * b)
                 bank = psum.tile([P, 512], F32, tag="bank", name="bank_%s%d_%d" % (op, r, b))
@@ -128,10 +128,10 @@ def tile_differentiablematcher_kernel(tc, pred_masks, gt_masks, out):
                 dst = gw[:, 512 * b : 512 * b + 256 * n].rearrange("p (s m u) -> p s m u", s=n, u=2)
                 src = bank[:, 0 : 256 * n].rearrange("p (s u m) -> p s m u", s=n, u=2)
                 if state["v"] < state["s"]:
-                    state["v"] += 4 * n + 1
+                    state["v"] += 8 * n + 2
                     nc.vector.tensor_copy(out=dst, in_=src)
                 else:
-                    state["s"] += 4 * n + 1
+                    state["s"] += 8 * n + 2
                     nc.scalar.copy(out=dst, in_=src)
             return g
 
@@ -197,9 +197,7 @@ def tile_differentiablematcher_kernel(tc, pred_masks, gt_masks, out):
                 quantise(waiting[0], waiting[1])
             waiting = (h, g)
         quantise(waiting[0], waiting[1])
-        mx_passes(len(ready) - state["issued"] - waiting[0][3])
-        dummy((512, 256))
-        mx_passes(waiting[0][3])
+        mx_passes(len(ready) - state["issued"])
         assert state["done"] == total_passes
 
         dummy((512, 256))
@@ -245,12 +243,12 @@ def tile_differentiablematcher_kernel(tc, pred_masks, gt_masks, out):
         for it in range(1, ITERS):
             a_ps = psum.tile([P, 1], F32, tag="bank", name="a_ps%d" % it)
             nc.tensor.matmul(a_ps[:], lhsT=kt[:], rhs=w[:], start=True, stop=True)
-            dummy((512, 256))
+            dummy((512,))
             u = small.tile([P, 1], F32, name="u%d" % it)
             nc.vector.reciprocal(out=u[:], in_=a_ps[:])
             c_ps = psum.tile([P, 1], F32, tag="bank", name="c_ps%d" % it)
             nc.tensor.matmul(c_ps[:], lhsT=kk[:], rhs=u[:], start=True, stop=True)
-            dummy((512, 256))
+            dummy((512,))
             w = small.tile([P, 1], F32, name="w%d" % it)
             nc.vector.reciprocal(out=w[:], in_=c_ps[:])
         wb = spread(w, "wb")

@@ -17,8 +17,8 @@ AX = mybir.AxisListType
 P = 128
 K_TOTAL = 65536
 PASS_K = 512
-CHUNKS = [16, 16, 16, 16, 16, 12, 8, 8, 6, 4, 4, 2, 2, 1, 1]
-X_SLOTS = 6
+CHUNKS = [24, 24, 20, 16, 12, 10, 8, 6, 4, 2, 1, 1]
+X_SLOTS = 4
 SMALL = 4
 GROUP_SIZES = (8, 4, 2, 1)
 CODE_BUFS = {("p", 8): 4, ("g", 8): 3}

from contextlib import ExitStack

import concourse.mybir as mybir
from concourse.masks import make_identity

FLOPS = 2 * 128 * 128 * 65536

F32 = mybir.dt.float32
BF16 = mybir.dt.bfloat16
U32 = mybir.dt.uint32
U8 = mybir.dt.uint8
FP8X4 = mybir.dt.float8_e4m3fn_x4
ALU = mybir.AluOpType
ACT = mybir.ActivationFunctionType
AX = mybir.AxisListType

P = 128
K_TOTAL = 65536
PASS_K = 512
CHUNKS = [24, 24, 20, 16, 12, 10, 8, 6, 4, 2, 1, 1]
X_SLOTS = 4
SMALL = 4
GROUP_SIZES = (8, 4, 2, 1)
CODE_BUFS = {("p", 8): 4, ("g", 8): 3}
MX_LAG_BANKS = 8
ITERS = 5


def tile_differentiablematcher_kernel(tc, pred_masks, gt_masks, out):
    nc = tc.nc
    srcs = {
        "p": pred_masks.rearrange("b k h w -> (b k) (h w)"),
        "g": gt_masks.rearrange("n h w -> n (h w)"),
    }
    out2 = out.rearrange("b k n -> (b k) n")
    total_passes = K_TOTAL // PASS_K
    assert sum(CHUNKS) == total_passes

    with ExitStack() as ctx:
        ctx.enter_context(tc.manual_schedule())
        const = ctx.enter_context(tc.tile_pool(name="const", bufs=1))
        xin = ctx.enter_context(tc.tile_pool(name="xin", bufs=X_SLOTS))
        grp = ctx.enter_context(tc.tile_pool(name="grp", bufs=4))
        cq = ctx.enter_context(tc.tile_pool(name="cq", bufs=3))
        mat = ctx.enter_context(tc.tile_pool(name="mat", bufs=1))
        small = ctx.enter_context(tc.tile_pool(name="small", bufs=1))
        psum = ctx.enter_context(tc.psum_pool(name="psum", bufs=7))
        accp = ctx.enter_context(tc.psum_pool(name="accp", bufs=1))

        starts = []
        k0 = 0
        for size in CHUNKS:
            starts.append(k0)
            k0 += size * PASS_K
        load_list = []
        for c in range(len(CHUNKS)):
            load_list.append(("p", c))
            load_list.append(("g", c))
        xt = {}
        state = {"next_load": 0, "banks": 0, "done": 0, "issued": 0, "s": 0, "v": 0, "dummies": 0}

        def load_one():
            i = state["next_load"]
            state["next_load"] = i + 1
            op, c = load_list[i]
            width = CHUNKS[c] * PASS_K
            if CHUNKS[c] > SMALL:
                x = xin.tile([P, width], BF16, tag="x", name="x_%s%d" % (op, c))
            else:
                x = xin.tile([P, width], BF16, tag="x_%s%d" % (op, c), bufs=1, name="x_%s%d" % (op, c))
            nc.sync.dma_start(out=x[:], in_=srcs[op][:, starts[c] : starts[c] + width])
            xt[(op, c)] = x

        def load_next():
            if state["next_load"] < len(load_list):
                load_one()
            while state["next_load"] < len(load_list) and CHUNKS[load_list[state["next_load"]][1]] <= SMALL:
                load_one()

        for i in range(X_SLOTS):
            load_next()

        ident = const.tile([P, P], F32, name="ident")
        make_identity(nc, ident[:])
        ones = const.tile([P, 1], F32, name="ones")
        nc.vector.memset(ones[:], 1.0)
        warm = const.tile([P, 1], F32, name="warm")
        nc.scalar.activation(out=warm[:], in_=ones[:], func=ACT.Exp)

        acc = accp.tile([P, P], F32, name="acc")
        dz = const.tile([P, 2048], BF16, name="dz", align_bytes=64)
        nc.vector.memset(dz[:], 1.0)
        dcodes = const.tile([P, 512], U32, name="dcodes", align_bytes=64)
        dscales = const.tile([P, 512], U8, name="dscales", align_bytes=64)
        nc.vector.quantize_mx(out=dcodes[:].bitcast(FP8X4), scales=dscales[:], in_=dz[:])

        groups = []
        n_ranges = 0
        for c in range(len(CHUNKS)):
            parts = []
            off = 0
            for q in GROUP_SIZES:
                while CHUNKS[c] - off >= q:
                    parts.append((off, q))
                    off += q
            for op in ("p", "g"):
                for j in range(len(parts)):
                    off, q = parts[j]
                    groups.append((op, c, off, q, n_ranges + j, j == len(parts) - 1))
            n_ranges += len(parts)

        quantised = {}
        ready = []

        def transposes(h):
            op, c, off, q, r, last = h
            g = grp.tile([P, q * PASS_K], BF16, tag="g", align_bytes=64, name="g_%s%d" % (op, r))
            gw = g[:].bitcast(F32)
            xw = xt[(op, c)][:].bitcast(F32)
            state["v"] += 5 * q + 2
            for b in range((q + 1) // 2):
                n = min(2, q - 2 * b)
                bank = psum.tile([P, 512], F32, tag="bank", name="bank_%s%d_%d" % (op, r, b))
                for j in range(2 * n):
                    col = 256 * (off + 2 * b) + 128 * j
                    nc.tensor.transpose(bank[:, 128 * j : 128 * j + 128], xw[:, col : col + 128], ident[:])
                state["banks"] += 1
                dst = gw[:, 512 * b : 512 * b + 256 * n].rearrange("p (s m u) -> p s m u", s=n, u=2)
                src = bank[:, 0 : 256 * n].rearrange("p (s u m) -> p s m u", s=n, u=2)
                if state["v"] < state["s"]:
                    state["v"] += 8 * n + 2
                    nc.vector.tensor_copy(out=dst, in_=src)
                else:
                    state["s"] += 8 * n + 2
                    nc.scalar.copy(out=dst, in_=src)
            return g

        def quantise(h, g):
            op, c, off, q, r, last = h
            bufs = CODE_BUFS.get((op, q), 3)
            codes = cq.tile(
                [P, q * P], U32, tag="c%s%d" % (op, q), bufs=bufs, align_bytes=64, name="c_%s%d" % (op, r)
            )
            scales = cq.tile(
                [P, q * P], U8, tag="s%s%d" % (op, q), bufs=bufs, align_bytes=64, name="s_%s%d" % (op, r)
            )
            nc.vector.quantize_mx(out=codes[:].bitcast(FP8X4), scales=scales[:], in_=g[:])
            quantised[(op, r)] = (codes, scales)
            if op == "g":
                for j in range(q):
                    ready.append((r, j, state["banks"]))

        def mx_passes(count):
            first = state["issued"]
            for r, j, b in ready[first : first + count]:
                cp, sp = quantised[("p", r)]
                cg, sg = quantised[("g", r)]
                cols = slice(P * j, P * j + P)
                n = state["done"]
                nc.tensor.matmul_mx(
                    out=acc[:],
                    lhsT=cp[:, cols].bitcast(FP8X4),
                    lhsT_scale=sp[:, cols],
                    rhs=cg[:, cols].bitcast(FP8X4),
                    rhs_scale=sg[:, cols],
                    start=(n == 0),
                    stop=(n == total_passes - 1),
                )
                state["done"] = n + 1
            state["issued"] = first + count

        def dummy(widths):
            state["dummies"] += 1
            scratch = psum.tile([P, 512], F32, tag="bank", name="scratch%d" % state["dummies"])
            for width in widths:
                nc.tensor.matmul_mx(
                    out=scratch[:, 0:width],
                    lhsT=dcodes[:, 0:128].bitcast(FP8X4),
                    lhsT_scale=dscales[:, 0:128],
                    rhs=dcodes[:, 0:width].bitcast(FP8X4),
                    rhs_scale=dscales[:, 0:width],
                    start=True,
                    stop=True,
                )

        waiting = None
        for h in groups:
            g = transposes(h)
            if h[5]:
                load_next()
            count = 0
            for r, j, b in ready[state["issued"] :]:
                if state["banks"] - b >= MX_LAG_BANKS:
                    count += 1
            mx_passes(count)
            if waiting is not None:
                quantise(waiting[0], waiting[1])
            waiting = (h, g)
        quantise(waiting[0], waiting[1])
        mx_passes(len(ready) - state["issued"])
        assert state["done"] == total_passes

        dummy((512, 256))

        def spread(vec, name):
            t = psum.tile([P, P], F32, tag="bank", name=name)
            nc.tensor.transpose(t[:], vec[:, 0:1].to_broadcast([P, P]), ident[:])
            return t

        m = small.tile([P, 1], F32, name="m")
        nc.vector.reduce_max(out=m[:], in_=acc[:], axis=AX.X)
        n1 = mat.tile([P, P], F32, name="n1")
        nc.vector.tensor_scalar(
            out=n1[:], in0=acc[:], scalar1=m[:, 0:1], scalar2=-10.0, op0=ALU.subtract, op1=ALU.mult
        )
        e1 = mat.tile([P, P], F32, name="e1")
        a1 = small.tile([P, 1], F32, name="a1")
        nc.scalar.activation(out=e1[:], in_=n1[:], func=ACT.Exp, scale=-1.0, accum_out=a1[:])
        n1t = psum.tile([P, P], F32, tag="bank", name="n1t")
        nc.tensor.transpose(n1t[:], n1[:], ident[:])
        dummy((512,))
        u = small.tile([P, 1], F32, name="u0")
        nc.vector.reciprocal(out=u[:], in_=a1[:])
        ub = spread(u, "ub")
        dummy((512,))
        mu = small.tile([P, 1], F32, name="mu")
        nc.vector.tensor_reduce(out=mu[:], in_=n1t[:], axis=AX.X, op=ALU.min)
        kt = mat.tile([P, P], F32, name="kt")
        nc.scalar.activation(out=kt[:], in_=n1t[:], func=ACT.Exp, bias=mu[:, 0:1], scale=-1.0)
        ktu = mat.tile([P, P], F32, name="ktu")
        c1 = small.tile([P, 1], F32, name="c1")
        nc.vector.scalar_tensor_tensor(
            out=ktu[:], in0=kt[:], scalar=1.0, in1=ub[:], op0=ALU.mult, op1=ALU.mult, accum_out=c1[:]
        )
        w = small.tile([P, 1], F32, name="w0")
        nc.vector.reciprocal(out=w[:], in_=c1[:])

        k_ps = psum.tile([P, P], F32, tag="bank", name="k_ps")
        nc.tensor.transpose(k_ps[:], kt[:], ident[:])
        dummy((512,))
        kk = mat.tile([P, P], F32, name="kk")
        nc.scalar.copy(out=kk[:], in_=k_ps[:])
        for it in range(1, ITERS):
            a_ps = psum.tile([P, 1], F32, tag="bank", name="a_ps%d" % it)
            nc.tensor.matmul(a_ps[:], lhsT=kt[:], rhs=w[:], start=True, stop=True)
            dummy((512,))
            u = small.tile([P, 1], F32, name="u%d" % it)
            nc.vector.reciprocal(out=u[:], in_=a_ps[:])
            c_ps = psum.tile([P, 1], F32, tag="bank", name="c_ps%d" % it)
            nc.tensor.matmul(c_ps[:], lhsT=kk[:], rhs=u[:], start=True, stop=True)
            dummy((512,))
            w = small.tile([P, 1], F32, name="w%d" % it)
            nc.vector.reciprocal(out=w[:], in_=c_ps[:])
        wb = spread(w, "wb")
        res = mat.tile([P, P], F32, name="res")
        nc.vector.scalar_tensor_tensor(
            out=res[:], in0=kk[:], scalar=u[:, 0:1], in1=wb[:], op0=ALU.mult, op1=ALU.mult
        )
        nc.sync.dma_start(out=out2, in_=res[:])
